import numpy as np
import ml_dtypes


def mxq(x, axis, fmt="e4m3"):
    dtype, down = {"e4m3": (ml_dtypes.float8_e4m3fn, 7), "e5m2": (ml_dtypes.float8_e5m2, 14)}[fmt]
    v = np.moveaxis(np.asarray(x, np.float32).astype(ml_dtypes.bfloat16).astype(np.float64), axis, -1)
    blocks = v.reshape(v.shape[:-1] + (-1, 32))
    amax = np.abs(blocks).max(-1, keepdims=True)
    byte = np.maximum(np.where(amax > 0, np.frexp(amax)[1] - 1 + 127, 0) - down, 1)
    scale = np.exp2(byte - 127.0)
    codes = (blocks / scale).astype(np.float32).astype(dtype).astype(np.float64)
    return np.moveaxis((codes * scale).reshape(v.shape), -1, axis)


WIDE = False


def mx_kscale(k):
    if not WIDE:
        return np.ones(k)
    levels = np.array([10, -10, 5, -5, 0])
    a = np.random.permutation(np.resize(levels, k // 512 * 4)).reshape(k // 512, 4)
    idx = np.arange(k)
    return np.exp2(a[idx // 512, idx % 128 // 32])


BF16 = ml_dtypes.bfloat16


def bf(x):
    return np.asarray(x, np.float32).astype(BF16)


def f64(x):
    return np.asarray(x).astype(np.float64)


B, D, U = 8192, 2048, 512
MASK_DENSITY = 1.0 / 16.0
W_STD = 1.0 / np.sqrt(U * MASK_DENSITY)


def setup_inputs():
    s, t = mx_kscale(U), mx_kscale(U)
    return {"h0": bf(np.random.standard_normal((B, U)) * s),
            "k1": bf(np.random.standard_normal((U, U)) * W_STD / s[:, None] * t),
            "k2": bf(np.random.standard_normal((U, U)) * W_STD / t[:, None]),
            "m1": bf(np.random.random((U, U)) < MASK_DENSITY),
            "m2": bf(np.random.random((U, U)) < MASK_DENSITY),
            "scaling": bf(np.random.uniform(1.25, 1.75, 1)),
            "bias": bf(np.random.standard_normal(U) * 0.5)}


def reference(h0, k1, k2, m1, m2, scaling, bias):
    w1 = f64(k1) * f64(m1)
    w2 = f64(k2) * f64(m2)
    h1 = mxq(f64(h0), 1, "e4m3") @ mxq(w1, 0, "e4m3")
    out = mxq(h1, 1, "e4m3") @ mxq(w2, 0, "e4m3")
    return np.maximum(f64(scaling) * out + f64(bias), 0.0)

@@ -1,0 +1,252 @@
+from contextlib import ExitStack
+
+import concourse.masks as masks
+import concourse.mybir as mybir
+
+F32 = mybir.dt.float32
+BF16 = mybir.dt.bfloat16
+U32 = mybir.dt.uint32
+U8 = mybir.dt.uint8
+FP8X4 = mybir.dt.float8_e4m3fn_x4
+ALU = mybir.AluOpType
+ACT = mybir.ActivationFunctionType
+
+P = 128
+ROWS = 8192
+U = 512
+TILES = ROWS // P
+GROUP = 4
+NG = TILES // GROUP
+GCOLS = GROUP * P
+FLT_MAX = 3.4028234663852886e38
+FLOPS = 2 * 2 * ROWS * U * U
+
+CHUNKS = [1, 1, 2, 4, 4, 4]
+LAG_A = 2
+LAG_G = 2
+MANUAL = True
+RELU = "GGGG"
+TAIL_SPLIT = 1
+
+
+def tile_sparsefactorisationdense_pa_t_kernel(tc, h0, k1, k2, m1, m2, scaling, bias, out):
+    nc = tc.nc
+    with ExitStack() as ctx:
+        const = ctx.enter_context(tc.tile_pool(name="const", bufs=1))
+        stage = ctx.enter_context(tc.tile_pool(name="stage", bufs=3))
+        quant = ctx.enter_context(tc.tile_pool(name="quant", bufs=4))
+        ypool = ctx.enter_context(tc.tile_pool(name="ypool", bufs=6))
+        tpool = ctx.enter_context(tc.psum_pool(name="tpool", bufs=2))
+        s1pool = ctx.enter_context(tc.psum_pool(name="s1pool", bufs=3))
+        s2pool = ctx.enter_context(tc.psum_pool(name="s2pool", bufs=3))
+        if MANUAL:
+            ctx.enter_context(tc.manual_schedule())
+
+        h0v = h0.rearrange("(p j) k -> p (j k)", j=TILES)
+        outv = out.rearrange("(p j) n -> p j n", j=TILES)
+
+        brow = const.tile([P, U + 64], BF16, name="brow")
+        ones = const.tile([P, P], BF16, name="ones")
+        nc.vector.memset(brow[:], 0.0)
+        nc.vector.memset(ones[:], 1.0)
+        nc.scalar.dma_start(out=brow[0:1, 0:U], in_=bias.rearrange("(o n) -> o n", o=1))
+        nc.scalar.dma_start(out=brow[0:1, U : U + 1], in_=scaling.rearrange("(o n) -> o n", o=1))
+        ident = const.tile([P, P], F32, name="ident")
+        masks.make_identity(nc, ident[:])
+
+        k1_sb = const.tile([P, 4 * U], BF16, name="k1_sb")
+        m1_sb = const.tile([P, 4 * U], BF16, name="m1_sb")
+        k2_sb = const.tile([P, 4 * U], BF16, name="k2_sb")
+        m2_sb = const.tile([P, 4 * U], BF16, name="m2_sb")
+
+        def load_w1(dst, src):
+            nc.sync.dma_start(
+                out=dst[:].rearrange("p (u x) -> p u x", u=2),
+                in_=src.rearrange("(u p e) c -> p u (e c)", u=2, e=2),
+            )
+
+        def load_w2(dst, src):
+            nc.sync.dma_start(out=dst[:], in_=src.rearrange("(p j) c -> p (j c)", j=4))
+
+        h0_tiles = []
+        group_src = []
+        g_first = 0
+        for c, n in enumerate(CHUNKS):
+            t = const.tile([P, n * GROUP * U], BF16, name="h0c%d" % c)
+            h0_tiles.append((t, g_first, n))
+            for i in range(n):
+                group_src.append((t, i))
+            g_first += n
+
+        def load_h0(c):
+            t, g_a, n = h0_tiles[c]
+            nc.sync.dma_start(out=t[:], in_=h0v[:, g_a * GROUP * U : (g_a + n) * GROUP * U])
+
+        load_w1(k1_sb, k1)
+        load_w1(m1_sb, m1)
+        load_h0(0)
+        load_h0(1)
+        load_w2(k2_sb, k2)
+        load_w2(m2_sb, m2)
+        for c in range(2, len(CHUNKS)):
+            load_h0(c)
+
+        bias_ps = s2pool.tile([P, U], F32, name="bias_ps", tag="s2")
+        nc.tensor.matmul(out=bias_ps[:], lhsT=ones[:], rhs=brow[:, 0:U], start=True, stop=True)
+        bias_f = const.tile([P, U], F32, name="bias_f")
+        nc.scalar.copy(out=bias_f[:], in_=bias_ps[:])
+        gain_ps = s2pool.tile([P, U], F32, name="gain_ps", tag="s2")
+        nc.tensor.matmul(out=gain_ps[:, 0:64], lhsT=ones[:], rhs=brow[:, U : U + 64], start=True, stop=True)
+        gain_f = const.tile([P, 1], F32, name="gain_f")
+        nc.scalar.copy(out=gain_f[:], in_=gain_ps[:, 0:1])
+
+        def quantise(src, name, pool):
+            codes = pool.tile([P, GCOLS], U32, name=name + "_c", tag=name + "_c", align_bytes=64)
+            scales = pool.tile([P, GCOLS], U8, name=name + "_s", tag=name + "_s", align_bytes=64)
+            nc.vector.quantize_mx(out=codes[:].bitcast(FP8X4), scales=scales[:], in_=src[:])
+            return codes, scales
+
+        def prepare_w1():
+            prod = const.tile([P, 4 * U], BF16, name="w1p")
+            nc.vector.tensor_tensor(out=prod[:], in0=k1_sb[:], in1=m1_sb[:], op=ALU.mult)
+            grouped = const.tile([P, 4 * U], BF16, name="w1g", align_bytes=64)
+            nc.vector.tensor_copy(
+                out=grouped[:].rearrange("p (s q t) -> p s q t", s=4, t=4),
+                in_=prod[:].rearrange("p (t q s) -> p s q t", t=4, s=4),
+            )
+            return quantise(grouped, "w1", const)
+
+        def prepare_w2():
+            prod = const.tile([P, 4 * U], BF16, name="w2p")
+            nc.vector.tensor_tensor(out=prod[:], in0=k2_sb[:], in1=m2_sb[:], op=ALU.mult)
+            grouped = const.tile([P, 4 * U], BF16, name="w2g", align_bytes=64)
+            nc.vector.tensor_copy(
+                out=grouped[:].rearrange("p (n j) -> p n j", j=4),
+                in_=prod[:].rearrange("p (j n) -> p n j", j=4),
+            )
+            return quantise(grouped, "w2", const)
+
+        g0_of = {}
+        q0_of = {}
+        g1_of = {}
+        q1_of = {}
+        y_of = {}
+
+        def transposes(g):
+            if g < 0 or g >= NG:
+                return
+            src, i = group_src[g]
+            words = src[:].bitcast(F32)
+            g0 = stage.tile([P, 4 * GCOLS], BF16, name="g0", tag="g0", align_bytes=64)
+            g0w = g0[:].bitcast(F32).rearrange("p (j r u) -> p j r u", j=GROUP, u=2)
+            for h in range(2):
+                tp = tpool.tile([P, 2, 2, P], F32, name="tp", tag="tp")
+                for jj in range(2):
+                    for u in range(2):
+                        w0 = (i * GROUP + 2 * h + jj) * (U // 2) + u * P
+                        nc.tensor.transpose(tp[:, jj, u, :], words[:, w0 : w0 + P], ident[:])
+                nc.scalar.copy(
+                    out=g0w[:, 2 * h : 2 * h + 2, :, :],
+                    in_=tp[:].rearrange("p j u r -> p j r u"),
+                )
+            g0_of[g] = g0
+
+        def quantise_h0(g):
+            if g < 0 or g >= NG:
+                return
+            q0_of[g] = quantise(g0_of[g], "q0", quant)
+
+        def stage1(g, jj):
+            if g < 0 or g >= NG:
+                return
+            if jj == 0:
+                g1_of[g] = stage.tile([P, 4 * GCOLS], BF16, name="g1", tag="g1", align_bytes=64)
+            g1v = g1_of[g][:].rearrange("p (j r t) -> p j r t", j=GROUP, t=4)
+            codes, scales = q0_of[g]
+            s1 = s1pool.tile([P, 4, P], F32, name="s1", tag="s1")
+            cols = slice(jj * P, (jj + 1) * P)
+            for t in range(4):
+                wcols = slice(t * P, (t + 1) * P)
+                nc.tensor.matmul_mx(
+                    out=s1[:, t, :],
+                    lhsT=w1c[:, wcols].bitcast(FP8X4),
+                    lhsT_scale=w1s[:, wcols],
+                    rhs=codes[:, cols].bitcast(FP8X4),
+                    rhs_scale=scales[:, cols],
+                    start=True,
+                    stop=True,
+                )
+            nc.scalar.copy(out=g1v[:, jj, :, :], in_=s1[:].rearrange("p t r -> p r t"))
+
+        def quantise_h1(g):
+            if g < 0 or g >= NG:
+                return
+            q1_of[g] = quantise(g1_of[g], "q1", quant)
+
+        def split_tail(g):
+            return g >= NG - TAIL_SPLIT
+
+        def stage2(g, jj):
+            if g < 0 or g >= NG:
+                return
+            if jj == 0:
+                y_of[g] = ypool.tile([P, GROUP, U], F32, name="y", tag="y")
+            y = y_of[g]
+            codes, scales = q1_of[g]
+            cols = slice(jj * P, (jj + 1) * P)
+            s2 = s2pool.tile([P, U], F32, name="s2", tag="s2")
+            nc.tensor.matmul_mx(
+                out=s2[:],
+                lhsT=codes[:, cols].bitcast(FP8X4),
+                lhsT_scale=scales[:, cols],
+                rhs=w2c[:].bitcast(FP8X4),
+                rhs_scale=w2s[:],
+                start=True,
+                stop=True,
+            )
+            nc.vector.scalar_tensor_tensor(
+                out=y[:, jj, :],
+                in0=s2[:],
+                scalar=gain_f[:, 0:1],
+                in1=bias_f[:],
+                op0=ALU.mult,
+                op1=ALU.add,
+            )
+            if split_tail(g):
+                nc.scalar.activation(out=y[:, jj, :], in_=y[:, jj, :], func=ACT.Relu)
+                nc.sync.dma_start(out=outv[:, g * GROUP + jj, :], in_=y[:, jj, :])
+
+        def relu_on(engine, ap):
+            if engine == "G":
+                nc.gpsimd.tensor_scalar(out=ap, in0=ap, scalar1=FLT_MAX, scalar2=0.0, op0=ALU.min, op1=ALU.max)
+            elif engine == "V":
+                nc.vector.tensor_scalar(out=ap, in0=ap, scalar1=0.0, scalar2=None, op0=ALU.max)
+            else:
+                nc.scalar.activation(out=ap, in_=ap, func=ACT.Relu)
+
+        def relu_store(g):
+            if g < 0 or g >= NG or split_tail(g):
+                return
+            y = y_of[g]
+            a = 0
+            while a < GROUP:
+                b = a + 1
+                while b < GROUP and RELU[b] == RELU[a]:
+                    b += 1
+                relu_on(RELU[a], y[:, a:b, :].rearrange("p j n -> p (j n)"))
+                a = b
+            nc.sync.dma_start(out=outv[:, g * GROUP : (g + 1) * GROUP, :], in_=y[:])
+
+        w1c, w1s = prepare_w1()
+        for g in range(LAG_A):
+            transposes(g)
+            quantise_h0(g)
+        w2c, w2s = prepare_w2()
+        for s in range(NG + LAG_G):
+            for jj in range(GROUP):
+                stage1(s, jj)
+                stage2(s - LAG_G, jj)
+            transposes(s + LAG_A)
+            relu_store(s - LAG_G)
+            quantise_h1(s)
+            quantise_h0(s + LAG_A)

@@ -25,8 +25,29 @@ CHUNKS = [1, 1, 2, 4, 4, 4]
 LAG_A = 2
 LAG_G = 2
 MANUAL = True
-RELU = "GGGG"
-TAIL_SPLIT = 1
+OFF = 0
+NK = NG + (1 if OFF else 0)
+Y_BUFS = 6
+
+
+def pattern(k):
+    return "SSSS" if k >= 14 else ("VVSS", "VVVS")[k % 2]
+
+
+def per_tile(k):
+    return k >= 14
+
+
+def e_engine(g, jj):
+    return "S"
+
+
+def b_engine(g, h):
+    return "S"
+
+
+def f_split(g):
+    return 1
 
 
 def tile_sparsefactorisationdense_pa_t_kernel(tc, h0, k1, k2, m1, m2, scaling, bias, out):
@@ -35,7 +56,7 @@ def tile_sparsefactorisationdense_pa_t_kernel(tc, h0, k1, k2, m1, m2, scaling, b
         const = ctx.enter_context(tc.tile_pool(name="const", bufs=1))
         stage = ctx.enter_context(tc.tile_pool(name="stage", bufs=3))
         quant = ctx.enter_context(tc.tile_pool(name="quant", bufs=4))
-        ypool = ctx.enter_context(tc.tile_pool(name="ypool", bufs=6))
+        ypool = ctx.enter_context(tc.tile_pool(name="ypool", bufs=Y_BUFS))
         tpool = ctx.enter_context(tc.psum_pool(name="tpool", bufs=2))
         s1pool = ctx.enter_context(tc.psum_pool(name="s1pool", bufs=3))
         s2pool = ctx.enter_context(tc.psum_pool(name="s2pool", bufs=3))
@@ -91,14 +112,16 @@ def tile_sparsefactorisationdense_pa_t_kernel(tc, h0, k1, k2, m1, m2, scaling, b
         for c in range(2, len(CHUNKS)):
             load_h0(c)
 
-        bias_ps = s2pool.tile([P, U], F32, name="bias_ps", tag="s2")
-        nc.tensor.matmul(out=bias_ps[:], lhsT=ones[:], rhs=brow[:, 0:U], start=True, stop=True)
+        def spread_bias():
+            bias_ps = s2pool.tile([P, U], F32, name="bias_ps", tag="s2")
+            nc.tensor.matmul(out=bias_ps[:], lhsT=ones[:], rhs=brow[:, 0:U], start=True, stop=True)
+            nc.scalar.copy(out=bias_f[:], in_=bias_ps[:])
+            gain_ps = s2pool.tile([P, U], F32, name="gain_ps", tag="s2")
+            nc.tensor.matmul(out=gain_ps[:, 0:64], lhsT=ones[:], rhs=brow[:, U : U + 64], start=True, stop=True)
+            nc.scalar.copy(out=gain_f[:], in_=gain_ps[:, 0:1])
+
         bias_f = const.tile([P, U], F32, name="bias_f")
-        nc.scalar.copy(out=bias_f[:], in_=bias_ps[:])
-        gain_ps = s2pool.tile([P, U], F32, name="gain_ps", tag="s2")
-        nc.tensor.matmul(out=gain_ps[:, 0:64], lhsT=ones[:], rhs=brow[:, U : U + 64], start=True, stop=True)
         gain_f = const.tile([P, 1], F32, name="gain_f")
-        nc.scalar.copy(out=gain_f[:], in_=gain_ps[:, 0:1])
 
         def quantise(src, name, pool):
             codes = pool.tile([P, GCOLS], U32, name=name + "_c", tag=name + "_c", align_bytes=64)
@@ -131,6 +154,15 @@ def tile_sparsefactorisationdense_pa_t_kernel(tc, h0, k1, k2, m1, m2, scaling, b
         g1_of = {}
         q1_of = {}
         y_of = {}
+        pending = {"V": [], "S": []}
+        stores = []
+        emitted = {}
+
+        def copy_on(engine, dst, src):
+            if engine == "S":
+                nc.scalar.copy(out=dst, in_=src)
+            else:
+                nc.vector.tensor_copy(out=dst, in_=src)
 
         def transposes(g):
             if g < 0 or g >= NG:
@@ -145,10 +177,7 @@ def tile_sparsefactorisationdense_pa_t_kernel(tc, h0, k1, k2, m1, m2, scaling, b
                     for u in range(2):
                         w0 = (i * GROUP + 2 * h + jj) * (U // 2) + u * P
                         nc.tensor.transpose(tp[:, jj, u, :], words[:, w0 : w0 + P], ident[:])
-                nc.scalar.copy(
-                    out=g0w[:, 2 * h : 2 * h + 2, :, :],
-                    in_=tp[:].rearrange("p j u r -> p j r u"),
-                )
+                copy_on(b_engine(g, h), g0w[:, 2 * h : 2 * h + 2, :, :], tp[:].rearrange("p j u r -> p j r u"))
             g0_of[g] = g0
 
         def quantise_h0(g):
@@ -176,22 +205,64 @@ def tile_sparsefactorisationdense_pa_t_kernel(tc, h0, k1, k2, m1, m2, scaling, b
                     start=True,
                     stop=True,
                 )
-            nc.scalar.copy(out=g1v[:, jj, :, :], in_=s1[:].rearrange("p t r -> p r t"))
+            copy_on(e_engine(g, jj), g1v[:, jj, :, :], s1[:].rearrange("p t r -> p r t"))
 
         def quantise_h1(g):
             if g < 0 or g >= NG:
                 return
-            q1_of[g] = quantise(g1_of[g], "q1", quant)
+            parts = f_split(g)
+            codes = quant.tile([P, GCOLS], U32, name="q1_c", tag="q1_c", align_bytes=64)
+            scales = quant.tile([P, GCOLS], U8, name="q1_s", tag="q1_s", align_bytes=64)
+            w = GCOLS // parts
+            for i in range(parts):
+                nc.vector.quantize_mx(
+                    out=codes[:, i * w : (i + 1) * w].bitcast(FP8X4),
+                    scales=scales[:, i * w : (i + 1) * w],
+                    in_=g1_of[g][:, 4 * i * w : 4 * (i + 1) * w],
+                )
+            q1_of[g] = (codes, scales)
 
-        def split_tail(g):
-            return g >= NG - TAIL_SPLIT
+        def slots(k):
+            return max(0, OFF - GROUP * k), min(GROUP, TILES - (GROUP * k - OFF))
+
+        def runs(k):
+            pat = pattern(k)
+            lo, hi = slots(k)
+            res = []
+            a = lo
+            while a < hi:
+                b = a + 1
+                while (not per_tile(k)) and b < hi and pat[b] == pat[a]:
+                    b += 1
+                res.append((pat[a], a, b))
+                a = b
+            return res
+
+        def relu(k, run):
+            engine, a, b = run
+            ap = y_of[k][:, a:b, :].rearrange("p j n -> p (j n)")
+            if engine == "G":
+                nc.gpsimd.tensor_scalar(out=ap, in0=ap, scalar1=FLT_MAX, scalar2=0.0, op0=ALU.min, op1=ALU.max)
+            elif engine == "V":
+                nc.vector.tensor_scalar(out=ap, in0=ap, scalar1=0.0, scalar2=None, op0=ALU.max)
+            else:
+                nc.scalar.activation(out=ap, in_=ap, func=ACT.Relu)
+            emitted[k] = emitted.get(k, 0) + 1
+            if per_tile(k):
+                stores.append((k, a, b))
+            elif emitted[k] == len(runs(k)):
+                lo, hi = slots(k)
+                stores.append((k, lo, hi))
 
         def stage2(g, jj):
             if g < 0 or g >= NG:
                 return
-            if jj == 0:
-                y_of[g] = ypool.tile([P, GROUP, U], F32, name="y", tag="y")
-            y = y_of[g]
+            tile_no = g * GROUP + jj
+            k = (tile_no + OFF) // GROUP
+            slot = (tile_no + OFF) % GROUP
+            if k not in y_of:
+                y_of[k] = ypool.tile([P, GROUP, U], F32, name="y", tag="y")
+            y = y_of[k]
             codes, scales = q1_of[g]
             cols = slice(jj * P, (jj + 1) * P)
             s2 = s2pool.tile([P, U], F32, name="s2", tag="s2")
@@ -205,48 +276,44 @@ def tile_sparsefactorisationdense_pa_t_kernel(tc, h0, k1, k2, m1, m2, scaling, b
                 stop=True,
             )
             nc.vector.scalar_tensor_tensor(
-                out=y[:, jj, :],
+                out=y[:, slot, :],
                 in0=s2[:],
                 scalar=gain_f[:, 0:1],
                 in1=bias_f[:],
                 op0=ALU.mult,
                 op1=ALU.add,
             )
-            if split_tail(g):
-                nc.scalar.activation(out=y[:, jj, :], in_=y[:, jj, :], func=ACT.Relu)
-                nc.sync.dma_start(out=outv[:, g * GROUP + jj, :], in_=y[:, jj, :])
+            for run in runs(k):
+                if run[2] - 1 == slot:
+                    if run[0] == "G":
+                        relu(k, run)
+                    else:
+                        pending[run[0]].append((k, run))
 
-        def relu_on(engine, ap):
-            if engine == "G":
-                nc.gpsimd.tensor_scalar(out=ap, in0=ap, scalar1=FLT_MAX, scalar2=0.0, op0=ALU.min, op1=ALU.max)
-            elif engine == "V":
-                nc.vector.tensor_scalar(out=ap, in0=ap, scalar1=0.0, scalar2=None, op0=ALU.max)
-            else:
-                nc.scalar.activation(out=ap, in_=ap, func=ACT.Relu)
+        def flush(engine):
+            for k, run in pending[engine]:
+                relu(k, run)
+            pending[engine] = []
 
-        def relu_store(g):
-            if g < 0 or g >= NG or split_tail(g):
-                return
-            y = y_of[g]
-            a = 0
-            while a < GROUP:
-                b = a + 1
-                while b < GROUP and RELU[b] == RELU[a]:
-                    b += 1
-                relu_on(RELU[a], y[:, a:b, :].rearrange("p j n -> p (j n)"))
-                a = b
-            nc.sync.dma_start(out=outv[:, g * GROUP : (g + 1) * GROUP, :], in_=y[:])
+        def store():
+            for k, a, b in stores:
+                first = GROUP * k - OFF
+                nc.sync.dma_start(out=outv[:, first + a : first + b, :], in_=y_of[k][:, a:b, :])
+            stores[:] = []
 
         w1c, w1s = prepare_w1()
         for g in range(LAG_A):
             transposes(g)
             quantise_h0(g)
+        spread_bias()
         w2c, w2s = prepare_w2()
         for s in range(NG + LAG_G):
             for jj in range(GROUP):
                 stage1(s, jj)
                 stage2(s - LAG_G, jj)
+            flush("V")
             transposes(s + LAG_A)
-            relu_store(s - LAG_G)
+            flush("S")
+            store()
             quantise_h1(s)
             quantise_h0(s + LAG_A)

@@ -19,6 +19,7 @@ GROUP = 4
 NG = TILES // GROUP
 GCOLS = GROUP * P
 FLT_MAX = 3.4028234663852886e38
+PAD = 8
 FLOPS = 2 * 2 * ROWS * U * U
 
 CHUNKS = [1, 1, 2, 4, 4, 4]
@@ -31,7 +32,7 @@ Y_BUFS = 6
 
 
 def pattern(k):
-    return "SSSS" if k >= 14 else ("VVSS", "VVVS")[k % 2]
+    return "SSSS" if k >= 14 else "TTTT"
 
 
 def per_tile(k):
@@ -154,7 +155,7 @@ def tile_sparsefactorisationdense_pa_t_kernel(tc, h0, k1, k2, m1, m2, scaling, b
         g1_of = {}
         q1_of = {}
         y_of = {}
-        pending = {"V": [], "S": []}
+        pending = {"V": [], "S": [], "T": []}
         stores = []
         emitted = {}
 
@@ -240,8 +241,12 @@ def tile_sparsefactorisationdense_pa_t_kernel(tc, h0, k1, k2, m1, m2, scaling, b
 
         def relu(k, run):
             engine, a, b = run
-            ap = y_of[k][:, a:b, :].rearrange("p j n -> p (j n)")
-            if engine == "G":
+            ap = y_of[k][:, a * U : b * U]
+            if engine == "T":
+                y = y_of[k]
+                nc.vector.memset(y[:, GROUP * U : GROUP * U + PAD], 0.0)
+                nc.gpsimd.tensor_scalar(out=y[:], in0=y[:], scalar1=FLT_MAX, scalar2=0.0, op0=ALU.min, op1=ALU.max)
+            elif engine == "G":
                 nc.gpsimd.tensor_scalar(out=ap, in0=ap, scalar1=FLT_MAX, scalar2=0.0, op0=ALU.min, op1=ALU.max)
             elif engine == "V":
                 nc.vector.tensor_scalar(out=ap, in0=ap, scalar1=0.0, scalar2=None, op0=ALU.max)
@@ -261,7 +266,7 @@ def tile_sparsefactorisationdense_pa_t_kernel(tc, h0, k1, k2, m1, m2, scaling, b
             k = (tile_no + OFF) // GROUP
             slot = (tile_no + OFF) % GROUP
             if k not in y_of:
-                y_of[k] = ypool.tile([P, GROUP, U], F32, name="y", tag="y")
+                y_of[k] = ypool.tile([P, GROUP * U + PAD], F32, name="y", tag="y")
             y = y_of[k]
             codes, scales = q1_of[g]
             cols = slice(jj * P, (jj + 1) * P)
@@ -276,7 +281,7 @@ def tile_sparsefactorisationdense_pa_t_kernel(tc, h0, k1, k2, m1, m2, scaling, b
                 stop=True,
             )
             nc.vector.scalar_tensor_tensor(
-                out=y[:, slot, :],
+                out=y[:, slot * U : (slot + 1) * U],
                 in0=s2[:],
                 scalar=gain_f[:, 0:1],
                 in1=bias_f[:],
@@ -298,7 +303,10 @@ def tile_sparsefactorisationdense_pa_t_kernel(tc, h0, k1, k2, m1, m2, scaling, b
         def store():
             for k, a, b in stores:
                 first = GROUP * k - OFF
-                nc.sync.dma_start(out=outv[:, first + a : first + b, :], in_=y_of[k][:, a:b, :])
+                nc.sync.dma_start(
+                    out=outv[:, first + a : first + b, :],
+                    in_=y_of[k][:, a * U : b * U].rearrange("p (j n) -> p j n", n=U),
+                )
             stores[:] = []
 
         w1c, w1s = prepare_w1()
@@ -317,3 +325,5 @@ def tile_sparsefactorisationdense_pa_t_kernel(tc, h0, k1, k2, m1, m2, scaling, b
             store()
             quantise_h1(s)
             quantise_h0(s + LAG_A)
+            flush("T")
+            store()

@@ -20,6 +20,7 @@ NG = TILES // GROUP
 GCOLS = GROUP * P
 FLT_MAX = 3.4028234663852886e38
 PAD = 8
+S_COLS = 256
 FLOPS = 2 * 2 * ROWS * U * U
 
 CHUNKS = [1, 1, 2, 4, 4, 4]
@@ -158,6 +159,7 @@ def tile_sparsefactorisationdense_pa_t_kernel(tc, h0, k1, k2, m1, m2, scaling, b
         pending = {"V": [], "S": [], "T": []}
         stores = []
         emitted = {}
+        head_relu = []
 
         def copy_on(engine, dst, src):
             if engine == "S":
@@ -245,7 +247,8 @@ def tile_sparsefactorisationdense_pa_t_kernel(tc, h0, k1, k2, m1, m2, scaling, b
             if engine == "T":
                 y = y_of[k]
                 nc.vector.memset(y[:, GROUP * U : GROUP * U + PAD], 0.0)
-                nc.gpsimd.tensor_scalar(out=y[:], in0=y[:], scalar1=FLT_MAX, scalar2=0.0, op0=ALU.min, op1=ALU.max)
+                rest = y[:, S_COLS:]
+                nc.gpsimd.tensor_scalar(out=rest, in0=rest, scalar1=FLT_MAX, scalar2=0.0, op0=ALU.min, op1=ALU.max)
             elif engine == "G":
                 nc.gpsimd.tensor_scalar(out=ap, in0=ap, scalar1=FLT_MAX, scalar2=0.0, op0=ALU.min, op1=ALU.max)
             elif engine == "V":
@@ -288,12 +291,20 @@ def tile_sparsefactorisationdense_pa_t_kernel(tc, h0, k1, k2, m1, m2, scaling, b
                 op0=ALU.mult,
                 op1=ALU.add,
             )
+            if pattern(k) == "TTTT" and slot == 0 and S_COLS:
+                head_relu.append(k)
             for run in runs(k):
                 if run[2] - 1 == slot:
                     if run[0] == "G":
                         relu(k, run)
                     else:
                         pending[run[0]].append((k, run))
+
+        def flush_head_relu():
+            for k in head_relu:
+                ap = y_of[k][:, 0:S_COLS]
+                nc.scalar.activation(out=ap, in_=ap, func=ACT.Relu)
+            head_relu[:] = []
 
         def flush(engine):
             for k, run in pending[engine]:
@@ -322,6 +333,7 @@ def tile_sparsefactorisationdense_pa_t_kernel(tc, h0, k1, k2, m1, m2, scaling, b
             flush("V")
             transposes(s + LAG_A)
             flush("S")
+            flush_head_relu()
             store()
             quantise_h1(s)
             quantise_h0(s + LAG_A)

@@ -24,7 +24,8 @@ S_COLS = 256
 FLOPS = 2 * 2 * ROWS * U * U
 
 CHUNKS = [1, 1, 2, 4, 4, 4]
-LAG_A = 2
+LAG_A = 3
+LAG_C = 2
 LAG_G = 2
 MANUAL = True
 OFF = 0
@@ -33,11 +34,11 @@ Y_BUFS = 6
 
 
 def pattern(k):
-    return "SSSS" if k >= 14 else "TTTT"
+    return "SSSS" if k >= 12 else "TTTT"
 
 
 def per_tile(k):
-    return k >= 14
+    return k >= 12
 
 
 def e_engine(g, jj):
@@ -56,8 +57,8 @@ def tile_sparsefactorisationdense_pa_t_kernel(tc, h0, k1, k2, m1, m2, scaling, b
     nc = tc.nc
     with ExitStack() as ctx:
         const = ctx.enter_context(tc.tile_pool(name="const", bufs=1))
-        stage = ctx.enter_context(tc.tile_pool(name="stage", bufs=3))
-        quant = ctx.enter_context(tc.tile_pool(name="quant", bufs=4))
+        stage = ctx.enter_context(tc.tile_pool(name="stage", bufs=4))
+        quant = ctx.enter_context(tc.tile_pool(name="quant", bufs=5))
         ypool = ctx.enter_context(tc.tile_pool(name="ypool", bufs=Y_BUFS))
         tpool = ctx.enter_context(tc.psum_pool(name="tpool", bufs=2))
         s1pool = ctx.enter_context(tc.psum_pool(name="s1pool", bufs=3))
@@ -72,8 +73,11 @@ def tile_sparsefactorisationdense_pa_t_kernel(tc, h0, k1, k2, m1, m2, scaling, b
         ones = const.tile([P, P], BF16, name="ones")
         nc.vector.memset(brow[:], 0.0)
         nc.vector.memset(ones[:], 1.0)
+        warm = const.tile([P, 8], F32, name="warm")
+        nc.vector.memset(warm[:], 0.0)
         nc.scalar.dma_start(out=brow[0:1, 0:U], in_=bias.rearrange("(o n) -> o n", o=1))
         nc.scalar.dma_start(out=brow[0:1, U : U + 1], in_=scaling.rearrange("(o n) -> o n", o=1))
+        nc.scalar.activation(out=warm[:], in_=warm[:], func=ACT.Relu)
         ident = const.tile([P, P], F32, name="ident")
         masks.make_identity(nc, ident[:])
 
@@ -109,9 +113,10 @@ def tile_sparsefactorisationdense_pa_t_kernel(tc, h0, k1, k2, m1, m2, scaling, b
         load_w1(m1_sb, m1)
         load_h0(0)
         load_h0(1)
+        load_h0(2)
         load_w2(k2_sb, k2)
         load_w2(m2_sb, m2)
-        for c in range(2, len(CHUNKS)):
+        for c in range(3, len(CHUNKS)):
             load_h0(c)
 
         def spread_bias():
@@ -323,6 +328,7 @@ def tile_sparsefactorisationdense_pa_t_kernel(tc, h0, k1, k2, m1, m2, scaling, b
         w1c, w1s = prepare_w1()
         for g in range(LAG_A):
             transposes(g)
+        for g in range(LAG_C):
             quantise_h0(g)
         spread_bias()
         w2c, w2s = prepare_w2()
@@ -336,6 +342,6 @@ def tile_sparsefactorisationdense_pa_t_kernel(tc, h0, k1, k2, m1, m2, scaling, b
             flush_head_relu()
             store()
             quantise_h1(s)
-            quantise_h0(s + LAG_A)
+            quantise_h0(s + LAG_C)
             flush("T")
             store()

@@ -20,6 +20,7 @@ NG = TILES // GROUP
 GCOLS = GROUP * P
 FLT_MAX = 3.4028234663852886e38
 PAD = 8
+STORE_TILES = 2
 S_COLS = 256
 FLOPS = 2 * 2 * ROWS * U * U
 
@@ -122,10 +123,10 @@ def tile_sparsefactorisationdense_pa_t_kernel(tc, h0, k1, k2, m1, m2, scaling, b
         def spread_bias():
             bias_ps = s2pool.tile([P, U], F32, name="bias_ps", tag="s2")
             nc.tensor.matmul(out=bias_ps[:], lhsT=ones[:], rhs=brow[:, 0:U], start=True, stop=True)
-            nc.scalar.copy(out=bias_f[:], in_=bias_ps[:])
+            nc.vector.tensor_copy(out=bias_f[:], in_=bias_ps[:])
             gain_ps = s2pool.tile([P, U], F32, name="gain_ps", tag="s2")
             nc.tensor.matmul(out=gain_ps[:, 0:64], lhsT=ones[:], rhs=brow[:, U : U + 64], start=True, stop=True)
-            nc.scalar.copy(out=gain_f[:], in_=gain_ps[:, 0:1])
+            nc.vector.tensor_copy(out=gain_f[:], in_=gain_ps[:, 0:1])
 
         bias_f = const.tile([P, U], F32, name="bias_f")
         gain_f = const.tile([P, 1], F32, name="gain_f")
@@ -262,7 +263,8 @@ def tile_sparsefactorisationdense_pa_t_kernel(tc, h0, k1, k2, m1, m2, scaling, b
                 nc.scalar.activation(out=ap, in_=ap, func=ACT.Relu)
             emitted[k] = emitted.get(k, 0) + 1
             if per_tile(k):
-                stores.append((k, a, b))
+                if b % STORE_TILES == 0:
+                    stores.append((k, b - STORE_TILES, b))
             elif emitted[k] == len(runs(k)):
                 lo, hi = slots(k)
                 stores.append((k, lo, hi))

from contextlib import ExitStack

import concourse.masks as masks
import concourse.mybir as mybir

F32 = mybir.dt.float32
BF16 = mybir.dt.bfloat16
U32 = mybir.dt.uint32
U8 = mybir.dt.uint8
FP8X4 = mybir.dt.float8_e4m3fn_x4
ALU = mybir.AluOpType
ACT = mybir.ActivationFunctionType

P = 128
ROWS = 8192
U = 512
TILES = ROWS // P
GROUP = 4
NG = TILES // GROUP
GCOLS = GROUP * P
FLT_MAX = 3.4028234663852886e38
PAD = 8
STORE_TILES = 2
S_COLS = 256
FLOPS = 2 * 2 * ROWS * U * U

CHUNKS = [1, 1, 2, 4, 4, 4]
LAG_A = 3
LAG_C = 2
LAG_G = 2
MANUAL = True
OFF = 0
NK = NG + (1 if OFF else 0)
Y_BUFS = 6


def pattern(k):
    return "SSSS" if k >= 12 else "TTTT"


def per_tile(k):
    return k >= 12


def e_engine(g, jj):
    return "S"


def b_engine(g, h):
    return "S"


def f_split(g):
    return 1


def tile_sparsefactorisationdense_pa_t_kernel(tc, h0, k1, k2, m1, m2, scaling, bias, out):
    nc = tc.nc
    with ExitStack() as ctx:
        const = ctx.enter_context(tc.tile_pool(name="const", bufs=1))
        stage = ctx.enter_context(tc.tile_pool(name="stage", bufs=4))
        quant = ctx.enter_context(tc.tile_pool(name="quant", bufs=5))
        ypool = ctx.enter_context(tc.tile_pool(name="ypool", bufs=Y_BUFS))
        tpool = ctx.enter_context(tc.psum_pool(name="tpool", bufs=2))
        s1pool = ctx.enter_context(tc.psum_pool(name="s1pool", bufs=3))
        s2pool = ctx.enter_context(tc.psum_pool(name="s2pool", bufs=3))
        if MANUAL:
            ctx.enter_context(tc.manual_schedule())

        h0v = h0.rearrange("(p j) k -> p (j k)", j=TILES)
        outv = out.rearrange("(p j) n -> p j n", j=TILES)

        brow = const.tile([P, U + 64], BF16, name="brow")
        ones = const.tile([P, P], BF16, name="ones")
        nc.vector.memset(brow[:], 0.0)
        nc.vector.memset(ones[:], 1.0)
        warm = const.tile([P, 8], F32, name="warm")
        nc.vector.memset(warm[:], 0.0)
        nc.scalar.dma_start(out=brow[0:1, 0:U], in_=bias.rearrange("(o n) -> o n", o=1))
        nc.scalar.dma_start(out=brow[0:1, U : U + 1], in_=scaling.rearrange("(o n) -> o n", o=1))
        nc.scalar.activation(out=warm[:], in_=warm[:], func=ACT.Relu)
        ident = const.tile([P, P], F32, name="ident")
        masks.make_identity(nc, ident[:])

        k1_sb = const.tile([P, 4 * U], BF16, name="k1_sb")
        m1_sb = const.tile([P, 4 * U], BF16, name="m1_sb")
        k2_sb = const.tile([P, 4 * U], BF16, name="k2_sb")
        m2_sb = const.tile([P, 4 * U], BF16, name="m2_sb")

        def load_w1(dst, src):
            nc.sync.dma_start(
                out=dst[:].rearrange("p (u x) -> p u x", u=2),
                in_=src.rearrange("(u p e) c -> p u (e c)", u=2, e=2),
            )

        def load_w2(dst, src):
            nc.sync.dma_start(out=dst[:], in_=src.rearrange("(p j) c -> p (j c)", j=4))

        h0_tiles = []
        group_src = []
        g_first = 0
        for c, n in enumerate(CHUNKS):
            t = const.tile([P, n * GROUP * U], BF16, name="h0c%d" % c)
            h0_tiles.append((t, g_first, n))
            for i in range(n):
                group_src.append((t, i))
            g_first += n

        def load_h0(c):
            t, g_a, n = h0_tiles[c]
            nc.sync.dma_start(out=t[:], in_=h0v[:, g_a * GROUP * U : (g_a + n) * GROUP * U])

        load_w1(k1_sb, k1)
        load_w1(m1_sb, m1)
        load_h0(0)
        load_h0(1)
        load_h0(2)
        load_w2(k2_sb, k2)
        load_w2(m2_sb, m2)
        for c in range(3, len(CHUNKS)):
            load_h0(c)

        def spread_bias():
            bias_ps = s2pool.tile([P, U], F32, name="bias_ps", tag="s2")
            nc.tensor.matmul(out=bias_ps[:], lhsT=ones[:], rhs=brow[:, 0:U], start=True, stop=True)
            nc.vector.tensor_copy(out=bias_f[:], in_=bias_ps[:])
            gain_ps = s2pool.tile([P, U], F32, name="gain_ps", tag="s2")
            nc.tensor.matmul(out=gain_ps[:, 0:64], lhsT=ones[:], rhs=brow[:, U : U + 64], start=True, stop=True)
            nc.vector.tensor_copy(out=gain_f[:], in_=gain_ps[:, 0:1])

        bias_f = const.tile([P, U], F32, name="bias_f")
        gain_f = const.tile([P, 1], F32, name="gain_f")

        def quantise(src, name, pool):
            codes = pool.tile([P, GCOLS], U32, name=name + "_c", tag=name + "_c", align_bytes=64)
            scales = pool.tile([P, GCOLS], U8, name=name + "_s", tag=name + "_s", align_bytes=64)
            nc.vector.quantize_mx(out=codes[:].bitcast(FP8X4), scales=scales[:], in_=src[:])
            return codes, scales

        def prepare_w1():
            prod = const.tile([P, 4 * U], BF16, name="w1p")
            nc.vector.tensor_tensor(out=prod[:], in0=k1_sb[:], in1=m1_sb[:], op=ALU.mult)
            grouped = const.tile([P, 4 * U], BF16, name="w1g", align_bytes=64)
            nc.vector.tensor_copy(
                out=grouped[:].rearrange("p (s q t) -> p s q t", s=4, t=4),
                in_=prod[:].rearrange("p (t q s) -> p s q t", t=4, s=4),
            )
            return quantise(grouped, "w1", const)

        def prepare_w2():
            prod = const.tile([P, 4 * U], BF16, name="w2p")
            nc.vector.tensor_tensor(out=prod[:], in0=k2_sb[:], in1=m2_sb[:], op=ALU.mult)
            grouped = const.tile([P, 4 * U], BF16, name="w2g", align_bytes=64)
            nc.vector.tensor_copy(
                out=grouped[:].rearrange("p (n j) -> p n j", j=4),
                in_=prod[:].rearrange("p (j n) -> p n j", j=4),
            )
            return quantise(grouped, "w2", const)

        g0_of = {}
        q0_of = {}
        g1_of = {}
        q1_of = {}
        y_of = {}
        pending = {"V": [], "S": [], "T": []}
        stores = []
        emitted = {}
        head_relu = []

        def copy_on(engine, dst, src):
            if engine == "S":
                nc.scalar.copy(out=dst, in_=src)
            else:
                nc.vector.tensor_copy(out=dst, in_=src)

        def transposes(g):
            if g < 0 or g >= NG:
                return
            src, i = group_src[g]
            words = src[:].bitcast(F32)
            g0 = stage.tile([P, 4 * GCOLS], BF16, name="g0", tag="g0", align_bytes=64)
            g0w = g0[:].bitcast(F32).rearrange("p (j r u) -> p j r u", j=GROUP, u=2)
            for h in range(2):
                tp = tpool.tile([P, 2, 2, P], F32, name="tp", tag="tp")
                for jj in range(2):
                    for u in range(2):
                        w0 = (i * GROUP + 2 * h + jj) * (U // 2) + u * P
                        nc.tensor.transpose(tp[:, jj, u, :], words[:, w0 : w0 + P], ident[:])
                copy_on(b_engine(g, h), g0w[:, 2 * h : 2 * h + 2, :, :], tp[:].rearrange("p j u r -> p j r u"))
            g0_of[g] = g0

        def quantise_h0(g):
            if g < 0 or g >= NG:
                return
            q0_of[g] = quantise(g0_of[g], "q0", quant)

        def stage1(g, jj):
            if g < 0 or g >= NG:
                return
            if jj == 0:
                g1_of[g] = stage.tile([P, 4 * GCOLS], BF16, name="g1", tag="g1", align_bytes=64)
            g1v = g1_of[g][:].rearrange("p (j r t) -> p j r t", j=GROUP, t=4)
            codes, scales = q0_of[g]
            s1 = s1pool.tile([P, 4, P], F32, name="s1", tag="s1")
            cols = slice(jj * P, (jj + 1) * P)
            for t in range(4):
                wcols = slice(t * P, (t + 1) * P)
                nc.tensor.matmul_mx(
                    out=s1[:, t, :],
                    lhsT=w1c[:, wcols].bitcast(FP8X4),
                    lhsT_scale=w1s[:, wcols],
                    rhs=codes[:, cols].bitcast(FP8X4),
                    rhs_scale=scales[:, cols],
                    start=True,
                    stop=True,
                )
            copy_on(e_engine(g, jj), g1v[:, jj, :, :], s1[:].rearrange("p t r -> p r t"))

        def quantise_h1(g):
            if g < 0 or g >= NG:
                return
            parts = f_split(g)
            codes = quant.tile([P, GCOLS], U32, name="q1_c", tag="q1_c", align_bytes=64)
            scales = quant.tile([P, GCOLS], U8, name="q1_s", tag="q1_s", align_bytes=64)
            w = GCOLS // parts
            for i in range(parts):
                nc.vector.quantize_mx(
                    out=codes[:, i * w : (i + 1) * w].bitcast(FP8X4),
                    scales=scales[:, i * w : (i + 1) * w],
                    in_=g1_of[g][:, 4 * i * w : 4 * (i + 1) * w],
                )
            q1_of[g] = (codes, scales)

        def slots(k):
            return max(0, OFF - GROUP * k), min(GROUP, TILES - (GROUP * k - OFF))

        def runs(k):
            pat = pattern(k)
            lo, hi = slots(k)
            res = []
            a = lo
            while a < hi:
                b = a + 1
                while (not per_tile(k)) and b < hi and pat[b] == pat[a]:
                    b += 1
                res.append((pat[a], a, b))
                a = b
            return res

        def relu(k, run):
            engine, a, b = run
            ap = y_of[k][:, a * U : b * U]
            if engine == "T":
                y = y_of[k]
                nc.vector.memset(y[:, GROUP * U : GROUP * U + PAD], 0.0)
                rest = y[:, S_COLS:]
                nc.gpsimd.tensor_scalar(out=rest, in0=rest, scalar1=FLT_MAX, scalar2=0.0, op0=ALU.min, op1=ALU.max)
            elif engine == "G":
                nc.gpsimd.tensor_scalar(out=ap, in0=ap, scalar1=FLT_MAX, scalar2=0.0, op0=ALU.min, op1=ALU.max)
            elif engine == "V":
                nc.vector.tensor_scalar(out=ap, in0=ap, scalar1=0.0, scalar2=None, op0=ALU.max)
            else:
                nc.scalar.activation(out=ap, in_=ap, func=ACT.Relu)
            emitted[k] = emitted.get(k, 0) + 1
            if per_tile(k):
                if b % STORE_TILES == 0:
                    stores.append((k, b - STORE_TILES, b))
            elif emitted[k] == len(runs(k)):
                lo, hi = slots(k)
                stores.append((k, lo, hi))

        def stage2(g, jj):
            if g < 0 or g >= NG:
                return
            tile_no = g * GROUP + jj
            k = (tile_no + OFF) // GROUP
            slot = (tile_no + OFF) % GROUP
            if k not in y_of:
                y_of[k] = ypool.tile([P, GROUP * U + PAD], F32, name="y", tag="y")
            y = y_of[k]
            codes, scales = q1_of[g]
            cols = slice(jj * P, (jj + 1) * P)
            s2 = s2pool.tile([P, U], F32, name="s2", tag="s2")
            nc.tensor.matmul_mx(
                out=s2[:],
                lhsT=codes[:, cols].bitcast(FP8X4),
                lhsT_scale=scales[:, cols],
                rhs=w2c[:].bitcast(FP8X4),
                rhs_scale=w2s[:],
                start=True,
                stop=True,
            )
            nc.vector.scalar_tensor_tensor(
                out=y[:, slot * U : (slot + 1) * U],
                in0=s2[:],
                scalar=gain_f[:, 0:1],
                in1=bias_f[:],
                op0=ALU.mult,
                op1=ALU.add,
            )
            if pattern(k) == "TTTT" and slot == 0 and S_COLS:
                head_relu.append(k)
            for run in runs(k):
                if run[2] - 1 == slot:
                    if run[0] == "G":
                        relu(k, run)
                    else:
                        pending[run[0]].append((k, run))

        def flush_head_relu():
            for k in head_relu:
                ap = y_of[k][:, 0:S_COLS]
                nc.scalar.activation(out=ap, in_=ap, func=ACT.Relu)
            head_relu[:] = []

        def flush(engine):
            for k, run in pending[engine]:
                relu(k, run)
            pending[engine] = []

        def store():
            for k, a, b in stores:
                first = GROUP * k - OFF
                nc.sync.dma_start(
                    out=outv[:, first + a : first + b, :],
                    in_=y_of[k][:, a * U : b * U].rearrange("p (j n) -> p j n", n=U),
                )
            stores[:] = []

        w1c, w1s = prepare_w1()
        for g in range(LAG_A):
            transposes(g)
        for g in range(LAG_C):
            quantise_h0(g)
        spread_bias()
        w2c, w2s = prepare_w2()
        for s in range(NG + LAG_G):
            for jj in range(GROUP):
                stage1(s, jj)
                stage2(s - LAG_G, jj)
            flush("V")
            transposes(s + LAG_A)
            flush("S")
            flush_head_relu()
            store()
            quantise_h1(s)
            quantise_h0(s + LAG_C)
            flush("T")
            store()
